import numpy as np
import ml_dtypes


BF16 = ml_dtypes.bfloat16


def bf(x):
    return np.asarray(x, np.float32).astype(BF16)


def f64(x):
    return np.asarray(x).astype(np.float64)


E2M1 = np.array([0.0, 0.5, 1.0, 1.5, 2.0, 3.0, 4.0, 6.0, -0.0, -0.5, -1.0, -1.5, -2.0, -3.0, -4.0, -6.0])


def pack_weight(w, fmt):
    k, n = w.shape
    w = f64(bf(w)).reshape(k // 32, 32, n)
    amax = np.abs(w).max(1)
    if fmt == "e4m3":
        byte = np.frexp(amax)[1] - 1 + 127 - 7
    else:
        mant, ex = np.frexp(amax / 6.0)
        byte = np.where(mant > 0.5, ex, ex - 1) + 127
    byte = np.clip(np.where(amax > 0, byte, 1), 1, 254)
    scaled = (w * np.exp2(127.0 - byte)[:, None, :]).reshape(k, n).astype(np.float32)
    by_word = np.ascontiguousarray(scaled.reshape(k // 512, 128, 4, n).transpose(0, 1, 3, 2))
    if fmt == "e4m3":
        words = by_word.astype(ml_dtypes.float8_e4m3fn).view(np.uint8)
    else:
        c = by_word.astype(ml_dtypes.float4_e2m1fn).view(np.uint8) & 0xF
        words = c[..., 0::2] | (c[..., 1::2] << 4)
    return np.ascontiguousarray(words), np.ascontiguousarray(byte.astype(np.uint8).reshape(k // 512, 16, n))


def unpack_weight(words, scales, fmt):
    g, p, n, _ = words.shape
    if fmt == "e4m3":
        vals = np.ascontiguousarray(words).view(ml_dtypes.float8_e4m3fn).astype(np.float64)
    else:
        nib = np.empty((g, p, n, 4), np.uint8)
        nib[..., 0::2] = words & 0xF
        nib[..., 1::2] = words >> 4
        vals = E2M1[nib]
    vals = vals * np.repeat(np.exp2(scales.astype(np.float64) - 127.0), 8, axis=1)[..., None]
    return vals.transpose(0, 1, 3, 2).reshape(g * 512, n)

def pack4(w):
    words, scales = pack_weight(w, "e2m1")
    return words.reshape(words.shape[0], 128, -1), scales


def unpack4(words, scales):
    return unpack_weight(words.reshape(words.shape[0], 128, -1, 2), scales, "e2m1")


def kspread(k):
    return np.exp2(np.repeat(np.random.randint(-6, 7, k // 32), 32).astype(np.float64))


B, D = 256, 3072


def softplus(v):
    return np.logaddexp(v, 0.0)


def setup_inputs():
    s = kspread(D)
    xt = np.random.standard_normal((B, D)) * 1.3 * s
    xt_words, xt_scales = pack4(xt.reshape(B, D).T)
    eps = bf(np.random.standard_normal((B, D)))
    x = bf(np.random.standard_normal((B, D)))
    t_rand = bf(np.random.uniform(0.0, 1.0, (B, 1)))
    Wm_words, Wm_scales = pack4((np.random.standard_normal((D, D)) / np.sqrt(D) / s[None, :]).T)
    bm = bf(np.random.standard_normal(D) * 0.5)
    Wv_words, Wv_scales = pack4((np.random.standard_normal((D, D)) / np.sqrt(D) / s[None, :]).T)
    bv = bf(np.random.standard_normal(D) * 0.5)
    return {"xt_words": xt_words, "xt_scales": xt_scales, "eps": eps, "x": x, "t_rand": t_rand,
            "Wm_words": Wm_words, "Wm_scales": Wm_scales, "bm": bm,
            "Wv_words": Wv_words, "Wv_scales": Wv_scales, "bv": bv}


def reference(xt_words, xt_scales, eps, x, t_rand, Wm_words, Wm_scales, bm, Wv_words, Wv_scales, bv):
    xq = unpack4(xt_words, xt_scales).T
    mu = (xq @ unpack4(Wm_words, Wm_scales)) + f64(bm)
    sigma = softplus((xq @ unpack4(Wv_words, Wv_scales)) + f64(bv))
    x_prime = mu + sigma * f64(eps)
    return (1.0 - f64(t_rand)) * f64(x) + f64(t_rand) * x_prime

@@ -1,0 +1,298 @@
+from contextlib import ExitStack
+
+import concourse.mybir as mybir
+from concourse.masks import make_identity
+
+B, D = 256, 3072
+FLOPS = 2 * B * D * (2 * D)
+
+F32 = mybir.dt.float32
+BF16 = mybir.dt.bfloat16
+U8 = mybir.dt.uint8
+I32 = mybir.dt.int32
+FP4X4 = mybir.dt.float4_e2m1fn_x4
+ACT = mybir.ActivationFunctionType
+ALU = mybir.AluOpType
+
+P = 128
+GROUPS = D // 512
+BLOCKS = B // P
+BANK = 512
+WIDE = 1024
+STRETCHES = D // WIDE
+CHUNKS = D // BANK
+SOFTPLUS_LINEAR = 40.0
+WARM_UP = 5
+
+
+def tile_diffscm_pb_kernel(
+    tc, xt_words, xt_scales, eps, x, t_rand, Wm_words, Wm_scales, bm, Wv_words, Wv_scales, bv, out
+):
+    nc = tc.nc
+    with ExitStack() as ctx:
+        keep = ctx.enter_context(tc.tile_pool(name="keep", bufs=1))
+        psum = ctx.enter_context(tc.psum_pool(name="psum", bufs=8))
+        ctx.enter_context(tc.manual_schedule())
+
+        weights = {"v": (Wv_words, Wv_scales), "m": (Wm_words, Wm_scales)}
+        planes = {}
+        codes = {}
+
+        def new_plane(head, s):
+            planes[head, s] = keep.tile([P, GROUPS, WIDE], U8, name="plane_%s%d" % (head, s), align_bytes=256)
+            return planes[head, s]
+
+        def load_codes(head, s, g0, g1):
+            part = keep.tile([P, g1 - g0, 2 * WIDE], U8, name="codes_%s%d_%d" % (head, s, g0), align_bytes=256)
+            src = weights[head][0][g0:g1, :, 2 * WIDE * s : 2 * WIDE * (s + 1)]
+            nc.sync.dma_start(out=part[:].bitcast(I32), in_=src.rearrange("g p n -> p g n").bitcast(I32))
+            for g in range(g0, g1):
+                codes[head, s, g] = (part, g - g0)
+
+        def load_scales(plane, scales):
+            for q in (0, 2, 1, 3):
+                src = scales[:, 4 * q : 4 * q + 4, :]
+                nc.sync.dma_start(
+                    out=plane[32 * q : 32 * q + 4, :, :].bitcast(I32),
+                    in_=src.rearrange("g r n -> r g n").bitcast(I32),
+                )
+
+        def load_weight_scales(head, s):
+            load_scales(planes[head, s], weights[head][1][:, :, WIDE * s : WIDE * (s + 1)])
+
+        bias_rows = keep.tile([P, BANK], BF16, name="bias_rows")
+        nc.gpsimd.memset(bias_rows[:].bitcast(F32), 0.0)
+        zeros = keep.tile([P, BANK], BF16, name="zeros")
+        nc.vector.memset(zeros[:], 0.0)
+        nc.scalar.dma_start(out=bias_rows[0:CHUNKS, :], in_=bm.rearrange("(c n) -> c n", n=BANK))
+        nc.scalar.dma_start(out=bias_rows[CHUNKS : 2 * CHUNKS, :], in_=bv.rearrange("(c n) -> c n", n=BANK))
+
+        xt_codes = keep.tile([P, GROUPS, 2 * B], U8, name="xt_codes", align_bytes=256)
+        nc.sync.dma_start(out=xt_codes[:].bitcast(I32), in_=xt_words.rearrange("g p n -> p g n").bitcast(I32))
+        load_codes("v", 0, 0, 1)
+        xt_plane = keep.tile([P, GROUPS, B], U8, name="xt_plane", align_bytes=256)
+        nc.vector.memset(xt_plane[:].bitcast(I32), 0)
+        load_scales(xt_plane, xt_scales)
+        nc.vector.memset(new_plane("v", 0)[:].bitcast(I32), 0)
+        load_weight_scales("v", 0)
+        load_codes("v", 0, 1, 2)
+        load_codes("v", 0, 2, 4)
+        load_codes("v", 0, 4, 6)
+
+        warm = keep.tile([P, 1], F32, name="warm")
+        nc.vector.memset(warm[:], 0.0)
+        nc.scalar.activation(out=warm[:], in_=warm[:], func=ACT.Exp)
+
+        ident = keep.tile([P, P], BF16, name="ident")
+        make_identity(nc, ident[:])
+
+        t_f32 = []
+        one_minus_t = []
+        for b in range(BLOCKS):
+            t_in = keep.tile([P, 1], BF16, name="t_in%d" % b)
+            nc.gpsimd.dma_start(out=t_in[:], in_=t_rand[P * b : P * (b + 1), :])
+            tf = keep.tile([P, 1], F32, name="t_f32_%d" % b)
+            nc.vector.tensor_copy(out=tf[:], in_=t_in[:])
+            om = keep.tile([P, 1], F32, name="one_minus_t_%d" % b)
+            nc.vector.tensor_scalar(out=om[:], in0=t_in[:], scalar1=-1.0, scalar2=1.0, op0=ALU.mult, op1=ALU.add)
+            t_f32.append(tf)
+            one_minus_t.append(om)
+
+        x_in = {}
+        eps_in = {}
+
+        def load_rows(store, src, s, name):
+            store[s] = keep.tile([P, BLOCKS, WIDE], BF16, name="%s%d" % (name, s))
+            nc.sync.dma_start(
+                out=store[s][:], in_=src[:, WIDE * s : WIDE * (s + 1)].rearrange("(b p) n -> p b n", p=P)
+            )
+
+        def load_weights(head, s):
+            load_codes(head, s, 0, 3)
+            load_codes(head, s, 3, 6)
+            load_weight_scales(head, s)
+
+        nc.vector.memset(new_plane("v", 1)[:].bitcast(I32), 0)
+        for head, s in (("v", 2), ("m", 0), ("m", 1), ("m", 2)):
+            nc.gpsimd.memset(new_plane(head, s)[:].bitcast(F32), 0.0)
+        load_rows(x_in, x, 0, "x")
+        load_rows(x_in, x, 1, "x")
+        load_weights("v", 1)
+        load_rows(x_in, x, 2, "x")
+        load_rows(eps_in, eps, 0, "eps")
+        load_weights("v", 2)
+        load_rows(eps_in, eps, 1, "eps")
+        load_weights("m", 0)
+        load_rows(eps_in, eps, 2, "eps")
+        load_weights("m", 1)
+        load_weights("m", 2)
+
+        warm_bank = psum.tile([P, BANK], F32, name="bank")
+        for w in range(WARM_UP):
+            nc.tensor.matmul(warm_bank[:], lhsT=zeros[:, 0:P], rhs=zeros[:], start=True, stop=True)
+
+        bias_all = {"m": keep.tile([P, D], BF16, name="bm_all"), "v": keep.tile([P, D], BF16, name="bv_all")}
+        for i in range(CHUNKS):
+            head, pair = ("m", i) if i < STRETCHES else ("v", i - STRETCHES)
+            bank = psum.tile([P, 2 * BANK], BF16, name="bank")
+            for h in range(2):
+                nc.tensor.matmul(
+                    bank[:, BANK * h : BANK * (h + 1)],
+                    lhsT=ident[:, 2 * i + h : 2 * i + h + 1].to_broadcast([P, P]),
+                    rhs=bias_rows[:],
+                    start=True,
+                    stop=True,
+                )
+            dst = bias_all[head][:, 2 * BANK * pair : 2 * BANK * (pair + 1)]
+            if i % 2 == 0:
+                nc.vector.tensor_copy(out=dst, in_=bank[:])
+            else:
+                nc.scalar.copy(out=dst, in_=bank[:])
+
+        acc = {}
+
+        def mx_pass(head, b, c0, c1, g):
+            s, lo = divmod(c0, WIDE)
+            hi = lo + c1 - c0
+            part, slot = codes[head, s, g]
+            nc.tensor.matmul_mx(
+                out=acc[head, b, c0][:, 0 : c1 - c0],
+                lhsT=xt_codes[:, g, 2 * P * b : 2 * P * (b + 1)].bitcast(FP4X4),
+                lhsT_scale=xt_plane[:, g, P * b : P * (b + 1)],
+                rhs=part[:, slot, 2 * lo : 2 * hi].bitcast(FP4X4),
+                rhs_scale=planes[head, s][:, g, lo:hi],
+                start=(g == 0),
+                stop=(g == GROUPS - 1),
+            )
+
+        def new_acc(head, b, c0, c1):
+            acc[head, b, c0] = psum.tile([P, BANK], F32, name="bank")
+
+        base = {}
+        v_pre = {}
+        soft = {}
+        for s in range(STRETCHES):
+            for b in range(BLOCKS):
+                base[s, b] = keep.tile([P, WIDE], F32, name="base%d%d" % (s, b))
+                v_pre[s, b] = keep.tile([P, WIDE], F32, name="v_pre%d%d" % (s, b))
+                soft[s, b] = keep.tile([P, WIDE], F32, name="soft%d%d" % (s, b))
+
+        def blend_x(s, b, on_scalar):
+            if on_scalar:
+                nc.scalar.activation(out=base[s, b][:], in_=x_in[s][:, b, :], func=ACT.Copy, scale=one_minus_t[b][:])
+            else:
+                nc.gpsimd.tensor_scalar(
+                    out=base[s, b][:], in0=x_in[s][:, b, :], scalar1=one_minus_t[b][:], scalar2=0.0,
+                    op0=ALU.mult, op1=ALU.add,
+                )
+
+        def blend_bm(s, b):
+            nc.vector.scalar_tensor_tensor(
+                out=base[s, b][:], in0=bias_all["m"][:, WIDE * s : WIDE * (s + 1)], scalar=t_f32[b][:],
+                in1=base[s, b][:], op0=ALU.mult, op1=ALU.add,
+            )
+
+        def add_bv(b, c0, c1):
+            s, lo = divmod(c0, WIDE)
+            nc.vector.tensor_tensor(
+                out=v_pre[s, b][:, lo : lo + c1 - c0], in0=acc["v", b, c0][:],
+                in1=bias_all["v"][:, c0:c1], op=ALU.add,
+            )
+
+        def exp_v(s, b):
+            nc.scalar.activation(out=soft[s, b][:], in_=v_pre[s, b][:], func=ACT.Exp)
+
+        def ln_v(s, b):
+            nc.scalar.activation(out=soft[s, b][:], in_=soft[s, b][:], func=ACT.Ln, bias=1.0)
+
+        def sigma(s, b):
+            nc.vector.scalar_tensor_tensor(
+                out=soft[s, b][:], in0=soft[s, b][:], scalar=SOFTPLUS_LINEAR, in1=v_pre[s, b][:],
+                op0=ALU.min, op1=ALU.max,
+            )
+
+        def noise(s, b):
+            nc.vector.scalar_tensor_tensor(
+                out=soft[s, b][:], in0=soft[s, b][:], scalar=t_f32[b][:], in1=eps_in[s][:, b, :],
+                op0=ALU.mult, op1=ALU.mult,
+            )
+
+        def gather(s, b):
+            for half in range(2):
+                cols = slice(BANK * half, BANK * (half + 1))
+                nc.gpsimd.tensor_tensor(
+                    out=base[s, b][:, cols], in0=soft[s, b][:, cols], in1=base[s, b][:, cols], op=ALU.add
+                )
+
+        def finish(b, c0, c1):
+            s, lo = divmod(c0, WIDE)
+            cols = slice(lo, lo + c1 - c0)
+            nc.vector.scalar_tensor_tensor(
+                out=base[s, b][:, cols], in0=acc["m", b, c0][:, 0 : c1 - c0], scalar=t_f32[b][:],
+                in1=base[s, b][:, cols], op0=ALU.mult, op1=ALU.add,
+            )
+            nc.sync.dma_start(out=out[P * b : P * (b + 1), c0:c1], in_=base[s, b][:, cols])
+
+        order = []
+        for head in "vm":
+            for s in range(STRETCHES):
+                for b in range(BLOCKS):
+                    for c0 in (WIDE * s, WIDE * s + BANK):
+                        order.append((head, b, c0, c0 + BANK))
+        head, b, c0, c1 = order.pop()
+        order += [(head, b, c0, c0 + BANK // 2), (head, b, c0 + BANK // 2, c1)]
+
+        for group in order[:4]:
+            new_acc(*group)
+        for g in range(GROUPS):
+            for group in order[:4]:
+                mx_pass(*group, g)
+
+        for s in (0, 1):
+            for b in range(BLOCKS):
+                blend_x(s, b, True)
+        for s in (0, 1):
+            for b in range(BLOCKS):
+                blend_bm(s, b)
+        blend_x(2, 0, False)
+        blend_x(2, 1, False)
+
+        fillers = {
+            6: [(blend_bm, 2, 0)],
+            7: [(blend_bm, 2, 1)],
+            8: [(sigma, 0, 0)],
+            9: [(sigma, 0, 1)],
+            10: [(noise, 0, 0), (gather, 0, 0)],
+            11: [(noise, 0, 1), (gather, 0, 1)],
+            13: [(sigma, 1, 0)],
+            14: [(noise, 1, 0), (gather, 1, 0)],
+            15: [(sigma, 1, 1)],
+            16: [(noise, 1, 1), (gather, 1, 1)],
+            18: [(sigma, 2, 0)],
+            19: [(noise, 2, 0), (gather, 2, 0)],
+            20: [(sigma, 2, 1)],
+            21: [(noise, 2, 1), (gather, 2, 1)],
+        }
+
+        def drain(j):
+            head, b, c0, c1 = order[j]
+            if head == "m":
+                finish(b, c0, c1)
+                return
+            add_bv(b, c0, c1)
+            s = c0 // WIDE
+            if c1 % WIDE == 0:
+                exp_v(s, b)
+                if b == 1:
+                    ln_v(s, 0)
+                    ln_v(s, 1)
+
+        for j in range(4, len(order) + 1):
+            if j < len(order):
+                new_acc(*order[j])
+                for g in range(GROUPS):
+                    mx_pass(*order[j], g)
+            for k in range(4) if j == 4 else (j - 1,):
+                drain(k)
+            for fill, s, b in fillers.get(j, ()):
+                fill(s, b)

@@ -20,9 +20,66 @@ BLOCKS = B // P
 BANK = 512
 WIDE = 1024
 STRETCHES = D // WIDE
-CHUNKS = D // BANK
 SOFTPLUS_LINEAR = 40.0
 WARM_UP = 5
+BIAS_ROWS = 8
+BIAS_COLS = D // BIAS_ROWS
+
+
+LOADS = (
+    "xt",
+    ("codes", "v", 0, 0, 1),
+    "xt scales",
+    ("scales", "v", 0),
+    ("codes", "v", 0, 1, 2),
+    ("x", 2),
+    ("x", 1),
+    ("codes", "v", 0, 2, 4),
+    ("codes", "v", 0, 4, 6),
+    ("codes", "v", 1, 0, 3),
+    ("x", 0),
+    ("scales", "v", 1),
+    ("codes", "v", 1, 3, 6),
+    ("codes", "v", 2, 3, 6),
+    ("scales", "v", 2),
+    ("codes", "v", 2, 0, 3),
+    ("eps", 0),
+    ("scales", "m", 0),
+    ("codes", "m", 0, 0, 3),
+    ("codes", "m", 0, 3, 6),
+    ("eps", 1),
+    ("eps", 2),
+    ("codes", "m", 1, 0, 3),
+    ("scales", "m", 1),
+    ("codes", "m", 1, 3, 6),
+    ("codes", "m", 2, 0, 3),
+    ("codes", "m", 2, 3, 6),
+    ("scales", "m", 2),
+)
+
+STEPS = {
+    3: "x11 x21 G11 x10 G21 x20 G10 A0 X00 x01 A1 A2 E00 A3",
+    4: "G20 E01 G00 L00",
+    5: "G01 A4 L01",
+    6: "C00 A5",
+    7: "C01 E10 A6",
+    8: "A7 D01 E11",
+    9: "D00 L11 A8",
+    10: "g00 A9",
+    11: "L10 C11 E20",
+    12: "C10 D11",
+    13: "A10 g11 A11",
+    14: "E21",
+    15: "L20 e01 D10",
+    16: "F12 g10 L21 F13",
+    17: "F14",
+    18: "C20 C21",
+    19: "D20",
+    20: "D21 F15 g20",
+    21: "F16 F17",
+    22: "F18 F19 g21 F20",
+    23: "F21 F22 F23",
+}
 
 
 def tile_diffscm_pb_kernel(
@@ -50,34 +107,27 @@ def tile_diffscm_pb_kernel(
                 codes[head, s, g] = (part, g - g0)
 
         def load_scales(plane, scales):
-            for q in (0, 2, 1, 3):
-                src = scales[:, 4 * q : 4 * q + 4, :]
+            for r in range(4):
                 nc.sync.dma_start(
-                    out=plane[32 * q : 32 * q + 4, :, :].bitcast(I32),
-                    in_=src.rearrange("g r n -> r g n").bitcast(I32),
+                    out=plane[r:P:32, :, :].bitcast(I32),
+                    in_=scales[:, r:16:4, :].rearrange("g q n -> q g n").bitcast(I32),
                 )
 
         def load_weight_scales(head, s):
             load_scales(planes[head, s], weights[head][1][:, :, WIDE * s : WIDE * (s + 1)])
 
-        bias_rows = keep.tile([P, BANK], BF16, name="bias_rows")
+        bias_rows = keep.tile([P, BIAS_COLS], BF16, name="bias_rows")
         nc.gpsimd.memset(bias_rows[:].bitcast(F32), 0.0)
         zeros = keep.tile([P, BANK], BF16, name="zeros")
         nc.vector.memset(zeros[:], 0.0)
-        nc.scalar.dma_start(out=bias_rows[0:CHUNKS, :], in_=bm.rearrange("(c n) -> c n", n=BANK))
-        nc.scalar.dma_start(out=bias_rows[CHUNKS : 2 * CHUNKS, :], in_=bv.rearrange("(c n) -> c n", n=BANK))
+        nc.scalar.dma_start(out=bias_rows[0:BIAS_ROWS, :], in_=bm.rearrange("(c n) -> c n", n=BIAS_COLS))
+        nc.scalar.dma_start(out=bias_rows[BIAS_ROWS : 2 * BIAS_ROWS, :], in_=bv.rearrange("(c n) -> c n", n=BIAS_COLS))
 
         xt_codes = keep.tile([P, GROUPS, 2 * B], U8, name="xt_codes", align_bytes=256)
-        nc.sync.dma_start(out=xt_codes[:].bitcast(I32), in_=xt_words.rearrange("g p n -> p g n").bitcast(I32))
-        load_codes("v", 0, 0, 1)
         xt_plane = keep.tile([P, GROUPS, B], U8, name="xt_plane", align_bytes=256)
         nc.vector.memset(xt_plane[:].bitcast(I32), 0)
-        load_scales(xt_plane, xt_scales)
         nc.vector.memset(new_plane("v", 0)[:].bitcast(I32), 0)
-        load_weight_scales("v", 0)
-        load_codes("v", 0, 1, 2)
-        load_codes("v", 0, 2, 4)
-        load_codes("v", 0, 4, 6)
+        nc.vector.memset(new_plane("v", 1)[:].bitcast(I32), 0)
 
         warm = keep.tile([P, 1], F32, name="warm")
         nc.vector.memset(warm[:], 0.0)
@@ -98,56 +148,52 @@ def tile_diffscm_pb_kernel(
             t_f32.append(tf)
             one_minus_t.append(om)
 
-        x_in = {}
-        eps_in = {}
-
-        def load_rows(store, src, s, name):
-            store[s] = keep.tile([P, BLOCKS, WIDE], BF16, name="%s%d" % (name, s))
-            nc.sync.dma_start(
-                out=store[s][:], in_=src[:, WIDE * s : WIDE * (s + 1)].rearrange("(b p) n -> p b n", p=P)
-            )
-
-        def load_weights(head, s):
-            load_codes(head, s, 0, 3)
-            load_codes(head, s, 3, 6)
-            load_weight_scales(head, s)
-
-        nc.vector.memset(new_plane("v", 1)[:].bitcast(I32), 0)
         for head, s in (("v", 2), ("m", 0), ("m", 1), ("m", 2)):
             nc.gpsimd.memset(new_plane(head, s)[:].bitcast(F32), 0.0)
-        load_rows(x_in, x, 0, "x")
-        load_rows(x_in, x, 1, "x")
-        load_weights("v", 1)
-        load_rows(x_in, x, 2, "x")
-        load_rows(eps_in, eps, 0, "eps")
-        load_weights("v", 2)
-        load_rows(eps_in, eps, 1, "eps")
-        load_weights("m", 0)
-        load_rows(eps_in, eps, 2, "eps")
-        load_weights("m", 1)
-        load_weights("m", 2)
+
+        rows = {}
+
+        def load_rows(name, s):
+            src = {"x": x, "eps": eps}[name][:, WIDE * s : WIDE * (s + 1)]
+            rows[name, s] = keep.tile([P, BLOCKS, WIDE], BF16, name="%s%d" % (name, s))
+            nc.sync.dma_start(out=rows[name, s][:], in_=src.rearrange("(b p) n -> p b n", p=P))
+
+        for item in LOADS:
+            if item == "xt":
+                nc.sync.dma_start(
+                    out=xt_codes[:].bitcast(I32), in_=xt_words.rearrange("g p n -> p g n").bitcast(I32)
+                )
+            elif item == "xt scales":
+                load_scales(xt_plane, xt_scales)
+            elif item[0] == "codes":
+                load_codes(*item[1:])
+            elif item[0] == "scales":
+                load_weight_scales(*item[1:])
+            else:
+                load_rows(*item)
 
         warm_bank = psum.tile([P, BANK], F32, name="bank")
         for w in range(WARM_UP):
             nc.tensor.matmul(warm_bank[:], lhsT=zeros[:, 0:P], rhs=zeros[:], start=True, stop=True)
 
         bias_all = {"m": keep.tile([P, D], BF16, name="bm_all"), "v": keep.tile([P, D], BF16, name="bv_all")}
-        for i in range(CHUNKS):
-            head, pair = ("m", i) if i < STRETCHES else ("v", i - STRETCHES)
-            bank = psum.tile([P, 2 * BANK], BF16, name="bank")
+        for i in range(BIAS_ROWS):
+            head, pair = ("m", i) if i < BIAS_ROWS // 2 else ("v", i - BIAS_ROWS // 2)
+            bank = psum.tile([P, 2, BANK], BF16, name="bank")
             for h in range(2):
                 nc.tensor.matmul(
-                    bank[:, BANK * h : BANK * (h + 1)],
+                    bank[:, h, 0:BIAS_COLS],
                     lhsT=ident[:, 2 * i + h : 2 * i + h + 1].to_broadcast([P, P]),
                     rhs=bias_rows[:],
                     start=True,
                     stop=True,
                 )
-            dst = bias_all[head][:, 2 * BANK * pair : 2 * BANK * (pair + 1)]
+            dst = bias_all[head][:, 2 * BIAS_COLS * pair : 2 * BIAS_COLS * (pair + 1)]
+            dst = dst.rearrange("p (h n) -> p h n", h=2)
             if i % 2 == 0:
-                nc.vector.tensor_copy(out=dst, in_=bank[:])
+                nc.vector.tensor_copy(out=dst, in_=bank[:, :, 0:BIAS_COLS])
             else:
-                nc.scalar.copy(out=dst, in_=bank[:])
+                nc.scalar.copy(out=dst, in_=bank[:, :, 0:BIAS_COLS])
 
         acc = {}
 
@@ -179,10 +225,10 @@ def tile_diffscm_pb_kernel(
 
         def blend_x(s, b, on_scalar):
             if on_scalar:
-                nc.scalar.activation(out=base[s, b][:], in_=x_in[s][:, b, :], func=ACT.Copy, scale=one_minus_t[b][:])
+                nc.scalar.activation(out=base[s, b][:], in_=rows["x", s][:, b, :], func=ACT.Copy, scale=one_minus_t[b][:])
             else:
                 nc.gpsimd.tensor_scalar(
-                    out=base[s, b][:], in0=x_in[s][:, b, :], scalar1=one_minus_t[b][:], scalar2=0.0,
+                    out=base[s, b][:], in0=rows["x", s][:, b, :], scalar1=one_minus_t[b][:], scalar2=0.0,
                     op0=ALU.mult, op1=ALU.add,
                 )
 
@@ -213,11 +259,14 @@ def tile_diffscm_pb_kernel(
 
         def noise(s, b):
             nc.vector.scalar_tensor_tensor(
-                out=soft[s, b][:], in0=soft[s, b][:], scalar=t_f32[b][:], in1=eps_in[s][:, b, :],
+                out=soft[s, b][:], in0=soft[s, b][:], scalar=t_f32[b][:], in1=rows["eps", s][:, b, :],
                 op0=ALU.mult, op1=ALU.mult,
             )
 
-        def gather(s, b):
+        def add_base(s, b, on_vector):
+            if on_vector:
+                nc.vector.tensor_tensor(out=base[s, b][:], in0=soft[s, b][:], in1=base[s, b][:], op=ALU.add)
+                return
             for half in range(2):
                 cols = slice(BANK * half, BANK * (half + 1))
                 nc.gpsimd.tensor_tensor(
@@ -238,61 +287,42 @@ def tile_diffscm_pb_kernel(
             for s in range(STRETCHES):
                 for b in range(BLOCKS):
                     for c0 in (WIDE * s, WIDE * s + BANK):
-                        order.append((head, b, c0, c0 + BANK))
-        head, b, c0, c1 = order.pop()
-        order += [(head, b, c0, c0 + BANK // 2), (head, b, c0 + BANK // 2, c1)]
+                        order.append([(head, b, c0, c0 + BANK)])
+        head, b, c0, c1 = order.pop()[0]
+        order.append([(head, b, c0, c0 + BANK // 2), (head, b, c0 + BANK // 2, c1)])
 
-        for group in order[:4]:
+        def run(token):
+            kind = token[0]
+            if kind in "AF":
+                for group in order[int(token[1:])]:
+                    (add_bv if kind == "A" else finish)(*group[1:])
+                return
+            s, b = int(token[1]), int(token[2])
+            if kind in "xX":
+                blend_x(s, b, kind == "x")
+            elif kind == "G":
+                blend_bm(s, b)
+            elif kind == "E":
+                exp_v(s, b)
+            elif kind == "L":
+                ln_v(s, b)
+            elif kind == "C":
+                sigma(s, b)
+            elif kind in "Dd":
+                noise(s, b)
+            else:
+                add_base(s, b, kind == "e")
+
+        for (group,) in order[:4]:
             new_acc(*group)
         for g in range(GROUPS):
-            for group in order[:4]:
+            for (group,) in order[:4]:
                 mx_pass(*group, g)
-
-        for s in (0, 1):
-            for b in range(BLOCKS):
-                blend_x(s, b, True)
-        for s in (0, 1):
-            for b in range(BLOCKS):
-                blend_bm(s, b)
-        blend_x(2, 0, False)
-        blend_x(2, 1, False)
-
-        fillers = {
-            6: [(blend_bm, 2, 0)],
-            7: [(blend_bm, 2, 1)],
-            8: [(sigma, 0, 0)],
-            9: [(sigma, 0, 1)],
-            10: [(noise, 0, 0), (gather, 0, 0)],
-            11: [(noise, 0, 1), (gather, 0, 1)],
-            13: [(sigma, 1, 0)],
-            14: [(noise, 1, 0), (gather, 1, 0)],
-            15: [(sigma, 1, 1)],
-            16: [(noise, 1, 1), (gather, 1, 1)],
-            18: [(sigma, 2, 0)],
-            19: [(noise, 2, 0), (gather, 2, 0)],
-            20: [(sigma, 2, 1)],
-            21: [(noise, 2, 1), (gather, 2, 1)],
-        }
-
-        def drain(j):
-            head, b, c0, c1 = order[j]
-            if head == "m":
-                finish(b, c0, c1)
-                return
-            add_bv(b, c0, c1)
-            s = c0 // WIDE
-            if c1 % WIDE == 0:
-                exp_v(s, b)
-                if b == 1:
-                    ln_v(s, 0)
-                    ln_v(s, 1)
-
-        for j in range(4, len(order) + 1):
-            if j < len(order):
-                new_acc(*order[j])
-                for g in range(GROUPS):
-                    mx_pass(*order[j], g)
-            for k in range(4) if j == 4 else (j - 1,):
-                drain(k)
-            for fill, s, b in fillers.get(j, ()):
-                fill(s, b)
+        for j in range(3, len(order)):
+            if j > 3:
+                for group in order[j]:
+                    new_acc(*group)
+                    for g in range(GROUPS):
+                        mx_pass(*group, g)
+            for token in STEPS[j].split():
+                run(token)

@@ -29,56 +29,56 @@ BIAS_COLS = D // BIAS_ROWS
 LOADS = (
     "xt",
     ("codes", "v", 0, 0, 1),
+    ("codes", "v", 0, 1, 2),
     "xt scales",
     ("scales", "v", 0),
-    ("codes", "v", 0, 1, 2),
     ("x", 2),
-    ("x", 1),
     ("codes", "v", 0, 2, 4),
-    ("codes", "v", 0, 4, 6),
-    ("codes", "v", 1, 0, 3),
     ("x", 0),
+    ("codes", "v", 0, 4, 6),
+    ("x", 1),
+    ("codes", "v", 1, 0, 3),
     ("scales", "v", 1),
     ("codes", "v", 1, 3, 6),
+    ("codes", "v", 2, 0, 3),
     ("codes", "v", 2, 3, 6),
     ("scales", "v", 2),
-    ("codes", "v", 2, 0, 3),
     ("eps", 0),
     ("scales", "m", 0),
     ("codes", "m", 0, 0, 3),
     ("codes", "m", 0, 3, 6),
     ("eps", 1),
-    ("eps", 2),
-    ("codes", "m", 1, 0, 3),
     ("scales", "m", 1),
+    ("codes", "m", 1, 0, 3),
     ("codes", "m", 1, 3, 6),
+    ("eps", 2),
+    ("scales", "m", 2),
     ("codes", "m", 2, 0, 3),
     ("codes", "m", 2, 3, 6),
-    ("scales", "m", 2),
 )
 
 STEPS = {
-    3: "x11 x21 G11 x10 G21 x20 G10 A0 X00 x01 A1 A2 E00 A3",
-    4: "G20 E01 G00 L00",
-    5: "G01 A4 L01",
-    6: "C00 A5",
-    7: "C01 E10 A6",
-    8: "A7 D01 E11",
-    9: "D00 L11 A8",
-    10: "g00 A9",
-    11: "L10 C11 E20",
-    12: "C10 D11",
-    13: "A10 g11 A11",
-    14: "E21",
-    15: "L20 e01 D10",
-    16: "F12 g10 L21 F13",
-    17: "F14",
-    18: "C20 C21",
-    19: "D20",
-    20: "D21 F15 g20",
-    21: "F16 F17",
-    22: "F18 F19 g21 F20",
-    23: "F21 F22 F23",
+    3: "X21 x20 G21 x00 G20 G00 x10 A0 X01 x11 A2 A1 A3 E00 G10",
+    4: "E01 G01 L00 G11",
+    5: "A4 L01",
+    6: "A5 C00 E10",
+    7: "A6 C01",
+    8: "A7 L10 D01",
+    9: "D00 E11",
+    10: "e01 C10",
+    11: "A9 w00 L11 A8",
+    12: "A10 A11",
+    13: "D10 E20 C11",
+    14: "D11",
+    15: "E21 e10 L20",
+    16: "F14 w11 F12",
+    17: "F16 L21 F13 C20",
+    18: "C21",
+    19: "D20 D21",
+    20: "F15 w20",
+    21: "F18 F17 F19",
+    22: "g21 F20 F21",
+    23: "F22 F23",
 }
 
 
@@ -263,13 +263,12 @@ def tile_diffscm_pb_kernel(
                 op0=ALU.mult, op1=ALU.mult,
             )
 
-        def add_base(s, b, on_vector):
-            if on_vector:
-                nc.vector.tensor_tensor(out=base[s, b][:], in0=soft[s, b][:], in1=base[s, b][:], op=ALU.add)
-                return
-            for half in range(2):
-                cols = slice(BANK * half, BANK * (half + 1))
-                nc.gpsimd.tensor_tensor(
+        def add_base(s, b, kind):
+            engine = nc.vector if kind == "e" else nc.gpsimd
+            width = BANK if kind == "g" else WIDE
+            for lo in range(0, WIDE, width):
+                cols = slice(lo, lo + width)
+                engine.tensor_tensor(
                     out=base[s, b][:, cols], in0=soft[s, b][:, cols], in1=base[s, b][:, cols], op=ALU.add
                 )
 
@@ -311,7 +310,7 @@ def tile_diffscm_pb_kernel(
             elif kind in "Dd":
                 noise(s, b)
             else:
-                add_base(s, b, kind == "e")
+                add_base(s, b, kind)
 
         for (group,) in order[:4]:
             new_acc(*group)

@@ -28,57 +28,57 @@ BIAS_COLS = D // BIAS_ROWS
 
 LOADS = (
     "xt",
-    ("codes", "v", 0, 0, 1),
-    ("codes", "v", 0, 1, 2),
-    "xt scales",
+    ("codes", "v", 0, 0, 1, 0, 2),
+    ("codes", "v", 0, 1, 2, 0, 2),
     ("scales", "v", 0),
     ("x", 2),
-    ("codes", "v", 0, 2, 4),
+    "xt scales",
+    ("codes", "v", 0, 2, 4, 0, 2),
     ("x", 0),
-    ("codes", "v", 0, 4, 6),
+    ("codes", "v", 0, 4, 6, 0, 2),
+    ("codes", "v", 1, 0, 6, 0, 1),
     ("x", 1),
-    ("codes", "v", 1, 0, 3),
     ("scales", "v", 1),
-    ("codes", "v", 1, 3, 6),
-    ("codes", "v", 2, 0, 3),
-    ("codes", "v", 2, 3, 6),
+    ("codes", "v", 1, 0, 6, 1, 2),
+    ("codes", "v", 2, 0, 6, 0, 1),
     ("scales", "v", 2),
+    ("codes", "v", 2, 0, 6, 1, 2),
     ("eps", 0),
     ("scales", "m", 0),
-    ("codes", "m", 0, 0, 3),
-    ("codes", "m", 0, 3, 6),
+    ("codes", "m", 0, 0, 6, 0, 1),
     ("eps", 1),
+    ("codes", "m", 0, 0, 6, 1, 2),
     ("scales", "m", 1),
-    ("codes", "m", 1, 0, 3),
-    ("codes", "m", 1, 3, 6),
+    ("codes", "m", 1, 0, 6, 0, 1),
     ("eps", 2),
+    ("codes", "m", 1, 0, 6, 1, 2),
     ("scales", "m", 2),
-    ("codes", "m", 2, 0, 3),
-    ("codes", "m", 2, 3, 6),
+    ("codes", "m", 2, 0, 6, 0, 1),
+    ("codes", "m", 2, 0, 6, 1, 2),
 )
 
 STEPS = {
-    3: "X21 x20 G21 x00 G20 G00 x10 A0 X01 x11 A2 A1 A3 E00 G10",
-    4: "E01 G01 L00 G11",
-    5: "A4 L01",
-    6: "A5 C00 E10",
-    7: "A6 C01",
-    8: "A7 L10 D01",
-    9: "D00 E11",
-    10: "e01 C10",
-    11: "A9 w00 L11 A8",
-    12: "A10 A11",
-    13: "D10 E20 C11",
-    14: "D11",
-    15: "E21 e10 L20",
-    16: "F14 w11 F12",
-    17: "F16 L21 F13 C20",
-    18: "C21",
-    19: "D20 D21",
-    20: "F15 w20",
-    21: "F18 F17 F19",
-    22: "g21 F20 F21",
-    23: "F22 F23",
+    3: "x20 x21 G20 G21 x01 x00 G01 G00 A0 X11 A2 A1 E00 X10 A3 E01",
+    4: "G10 L00",
+    5: "A4 G11",
+    6: "A5 L01 C00",
+    7: "A6 C01 E10",
+    8: "A7",
+    9: "E11 D01 L10",
+    10: "D00 e01 g00",
+    11: "A10 L11 A9",
+    12: "A8 A11",
+    13: "C10 E21 C11",
+    14: "D11 E20",
+    15: "D10 w11 L21 F14",
+    16: "F12 F15",
+    17: "L20 C21 e10",
+    18: "D21",
+    19: "C20 g21 F13",
+    20: "F18 D20",
+    21: "F17 w20 F19",
+    22: "F21 F16",
+    23: "F22 F20 F23",
 }
 
 
@@ -99,12 +99,16 @@ def tile_diffscm_pb_kernel(
             planes[head, s] = keep.tile([P, GROUPS, WIDE], U8, name="plane_%s%d" % (head, s), align_bytes=256)
             return planes[head, s]
 
-        def load_codes(head, s, g0, g1):
-            part = keep.tile([P, g1 - g0, 2 * WIDE], U8, name="codes_%s%d_%d" % (head, s, g0), align_bytes=256)
-            src = weights[head][0][g0:g1, :, 2 * WIDE * s : 2 * WIDE * (s + 1)]
+        def load_codes(head, s, g0, g1, h0, h1):
+            name = "codes_%s%d_%d%d" % (head, s, g0, h0)
+            part = keep.tile([P, g1 - g0, 2 * BANK * (h1 - h0)], U8, name=name, align_bytes=256)
+            c0 = WIDE * s + BANK * h0
+            c1 = WIDE * s + BANK * h1
+            src = weights[head][0][g0:g1, :, 2 * c0 : 2 * c1]
             nc.sync.dma_start(out=part[:].bitcast(I32), in_=src.rearrange("g p n -> p g n").bitcast(I32))
             for g in range(g0, g1):
-                codes[head, s, g] = (part, g - g0)
+                for h in range(h0, h1):
+                    codes[head, s, g, h] = part[:, g - g0, 2 * BANK * (h - h0) : 2 * BANK * (h - h0 + 1)]
 
         def load_scales(plane, scales):
             for r in range(4):
@@ -200,12 +204,12 @@ def tile_diffscm_pb_kernel(
         def mx_pass(head, b, c0, c1, g):
             s, lo = divmod(c0, WIDE)
             hi = lo + c1 - c0
-            part, slot = codes[head, s, g]
+            half, sub = divmod(lo, BANK)
             nc.tensor.matmul_mx(
                 out=acc[head, b, c0][:, 0 : c1 - c0],
                 lhsT=xt_codes[:, g, 2 * P * b : 2 * P * (b + 1)].bitcast(FP4X4),
                 lhsT_scale=xt_plane[:, g, P * b : P * (b + 1)],
-                rhs=part[:, slot, 2 * lo : 2 * hi].bitcast(FP4X4),
+                rhs=codes[head, s, g, half][:, 2 * sub : 2 * (sub + hi - lo)].bitcast(FP4X4),
                 rhs_scale=planes[head, s][:, g, lo:hi],
                 start=(g == 0),
                 stop=(g == GROUPS - 1),
@@ -284,8 +288,8 @@ def tile_diffscm_pb_kernel(
         order = []
         for head in "vm":
             for s in range(STRETCHES):
-                for b in range(BLOCKS):
-                    for c0 in (WIDE * s, WIDE * s + BANK):
+                for c0 in (WIDE * s, WIDE * s + BANK):
+                    for b in range(BLOCKS):
                         order.append([(head, b, c0, c0 + BANK)])
         head, b, c0, c1 = order.pop()[0]
         order.append([(head, b, c0, c0 + BANK // 2), (head, b, c0 + BANK // 2, c1)])

from contextlib import ExitStack

import concourse.mybir as mybir
from concourse.masks import make_identity

B, D = 256, 3072
FLOPS = 2 * B * D * (2 * D)

F32 = mybir.dt.float32
BF16 = mybir.dt.bfloat16
U8 = mybir.dt.uint8
I32 = mybir.dt.int32
FP4X4 = mybir.dt.float4_e2m1fn_x4
ACT = mybir.ActivationFunctionType
ALU = mybir.AluOpType

P = 128
GROUPS = D // 512
BLOCKS = B // P
BANK = 512
WIDE = 1024
STRETCHES = D // WIDE
SOFTPLUS_LINEAR = 40.0
WARM_UP = 5
BIAS_ROWS = 8
BIAS_COLS = D // BIAS_ROWS


LOADS = (
    "xt",
    ("codes", "v", 0, 0, 1, 0, 2),
    ("codes", "v", 0, 1, 2, 0, 2),
    ("scales", "v", 0),
    ("x", 2),
    "xt scales",
    ("codes", "v", 0, 2, 4, 0, 2),
    ("x", 0),
    ("codes", "v", 0, 4, 6, 0, 2),
    ("codes", "v", 1, 0, 6, 0, 1),
    ("x", 1),
    ("scales", "v", 1),
    ("codes", "v", 1, 0, 6, 1, 2),
    ("codes", "v", 2, 0, 6, 0, 1),
    ("scales", "v", 2),
    ("codes", "v", 2, 0, 6, 1, 2),
    ("eps", 0),
    ("scales", "m", 0),
    ("codes", "m", 0, 0, 6, 0, 1),
    ("eps", 1),
    ("codes", "m", 0, 0, 6, 1, 2),
    ("scales", "m", 1),
    ("codes", "m", 1, 0, 6, 0, 1),
    ("eps", 2),
    ("codes", "m", 1, 0, 6, 1, 2),
    ("scales", "m", 2),
    ("codes", "m", 2, 0, 6, 0, 1),
    ("codes", "m", 2, 0, 6, 1, 2),
)

STEPS = {
    3: "x20 x21 G20 G21 x01 x00 G01 G00 A0 X11 A2 A1 E00 X10 A3 E01",
    4: "G10 L00",
    5: "A4 G11",
    6: "A5 L01 C00",
    7: "A6 C01 E10",
    8: "A7",
    9: "E11 D01 L10",
    10: "D00 e01 g00",
    11: "A10 L11 A9",
    12: "A8 A11",
    13: "C10 E21 C11",
    14: "D11 E20",
    15: "D10 w11 L21 F14",
    16: "F12 F15",
    17: "L20 C21 e10",
    18: "D21",
    19: "C20 g21 F13",
    20: "F18 D20",
    21: "F17 w20 F19",
    22: "F21 F16",
    23: "F22 F20 F23",
}


def tile_diffscm_pb_kernel(
    tc, xt_words, xt_scales, eps, x, t_rand, Wm_words, Wm_scales, bm, Wv_words, Wv_scales, bv, out
):
    nc = tc.nc
    with ExitStack() as ctx:
        keep = ctx.enter_context(tc.tile_pool(name="keep", bufs=1))
        psum = ctx.enter_context(tc.psum_pool(name="psum", bufs=8))
        ctx.enter_context(tc.manual_schedule())

        weights = {"v": (Wv_words, Wv_scales), "m": (Wm_words, Wm_scales)}
        planes = {}
        codes = {}

        def new_plane(head, s):
            planes[head, s] = keep.tile([P, GROUPS, WIDE], U8, name="plane_%s%d" % (head, s), align_bytes=256)
            return planes[head, s]

        def load_codes(head, s, g0, g1, h0, h1):
            name = "codes_%s%d_%d%d" % (head, s, g0, h0)
            part = keep.tile([P, g1 - g0, 2 * BANK * (h1 - h0)], U8, name=name, align_bytes=256)
            c0 = WIDE * s + BANK * h0
            c1 = WIDE * s + BANK * h1
            src = weights[head][0][g0:g1, :, 2 * c0 : 2 * c1]
            nc.sync.dma_start(out=part[:].bitcast(I32), in_=src.rearrange("g p n -> p g n").bitcast(I32))
            for g in range(g0, g1):
                for h in range(h0, h1):
                    codes[head, s, g, h] = part[:, g - g0, 2 * BANK * (h - h0) : 2 * BANK * (h - h0 + 1)]

        def load_scales(plane, scales):
            for r in range(4):
                nc.sync.dma_start(
                    out=plane[r:P:32, :, :].bitcast(I32),
                    in_=scales[:, r:16:4, :].rearrange("g q n -> q g n").bitcast(I32),
                )

        def load_weight_scales(head, s):
            load_scales(planes[head, s], weights[head][1][:, :, WIDE * s : WIDE * (s + 1)])

        bias_rows = keep.tile([P, BIAS_COLS], BF16, name="bias_rows")
        nc.gpsimd.memset(bias_rows[:].bitcast(F32), 0.0)
        zeros = keep.tile([P, BANK], BF16, name="zeros")
        nc.vector.memset(zeros[:], 0.0)
        nc.scalar.dma_start(out=bias_rows[0:BIAS_ROWS, :], in_=bm.rearrange("(c n) -> c n", n=BIAS_COLS))
        nc.scalar.dma_start(out=bias_rows[BIAS_ROWS : 2 * BIAS_ROWS, :], in_=bv.rearrange("(c n) -> c n", n=BIAS_COLS))

        xt_codes = keep.tile([P, GROUPS, 2 * B], U8, name="xt_codes", align_bytes=256)
        xt_plane = keep.tile([P, GROUPS, B], U8, name="xt_plane", align_bytes=256)
        nc.vector.memset(xt_plane[:].bitcast(I32), 0)
        nc.vector.memset(new_plane("v", 0)[:].bitcast(I32), 0)
        nc.vector.memset(new_plane("v", 1)[:].bitcast(I32), 0)

        warm = keep.tile([P, 1], F32, name="warm")
        nc.vector.memset(warm[:], 0.0)
        nc.scalar.activation(out=warm[:], in_=warm[:], func=ACT.Exp)

        ident = keep.tile([P, P], BF16, name="ident")
        make_identity(nc, ident[:])

        t_f32 = []
        one_minus_t = []
        for b in range(BLOCKS):
            t_in = keep.tile([P, 1], BF16, name="t_in%d" % b)
            nc.gpsimd.dma_start(out=t_in[:], in_=t_rand[P * b : P * (b + 1), :])
            tf = keep.tile([P, 1], F32, name="t_f32_%d" % b)
            nc.vector.tensor_copy(out=tf[:], in_=t_in[:])
            om = keep.tile([P, 1], F32, name="one_minus_t_%d" % b)
            nc.vector.tensor_scalar(out=om[:], in0=t_in[:], scalar1=-1.0, scalar2=1.0, op0=ALU.mult, op1=ALU.add)
            t_f32.append(tf)
            one_minus_t.append(om)

        for head, s in (("v", 2), ("m", 0), ("m", 1), ("m", 2)):
            nc.gpsimd.memset(new_plane(head, s)[:].bitcast(F32), 0.0)

        rows = {}

        def load_rows(name, s):
            src = {"x": x, "eps": eps}[name][:, WIDE * s : WIDE * (s + 1)]
            rows[name, s] = keep.tile([P, BLOCKS, WIDE], BF16, name="%s%d" % (name, s))
            nc.sync.dma_start(out=rows[name, s][:], in_=src.rearrange("(b p) n -> p b n", p=P))

        for item in LOADS:
            if item == "xt":
                nc.sync.dma_start(
                    out=xt_codes[:].bitcast(I32), in_=xt_words.rearrange("g p n -> p g n").bitcast(I32)
                )
            elif item == "xt scales":
                load_scales(xt_plane, xt_scales)
            elif item[0] == "codes":
                load_codes(*item[1:])
            elif item[0] == "scales":
                load_weight_scales(*item[1:])
            else:
                load_rows(*item)

        warm_bank = psum.tile([P, BANK], F32, name="bank")
        for w in range(WARM_UP):
            nc.tensor.matmul(warm_bank[:], lhsT=zeros[:, 0:P], rhs=zeros[:], start=True, stop=True)

        bias_all = {"m": keep.tile([P, D], BF16, name="bm_all"), "v": keep.tile([P, D], BF16, name="bv_all")}
        for i in range(BIAS_ROWS):
            head, pair = ("m", i) if i < BIAS_ROWS // 2 else ("v", i - BIAS_ROWS // 2)
            bank = psum.tile([P, 2, BANK], BF16, name="bank")
            for h in range(2):
                nc.tensor.matmul(
                    bank[:, h, 0:BIAS_COLS],
                    lhsT=ident[:, 2 * i + h : 2 * i + h + 1].to_broadcast([P, P]),
                    rhs=bias_rows[:],
                    start=True,
                    stop=True,
                )
            dst = bias_all[head][:, 2 * BIAS_COLS * pair : 2 * BIAS_COLS * (pair + 1)]
            dst = dst.rearrange("p (h n) -> p h n", h=2)
            if i % 2 == 0:
                nc.vector.tensor_copy(out=dst, in_=bank[:, :, 0:BIAS_COLS])
            else:
                nc.scalar.copy(out=dst, in_=bank[:, :, 0:BIAS_COLS])

        acc = {}

        def mx_pass(head, b, c0, c1, g):
            s, lo = divmod(c0, WIDE)
            hi = lo + c1 - c0
            half, sub = divmod(lo, BANK)
            nc.tensor.matmul_mx(
                out=acc[head, b, c0][:, 0 : c1 - c0],
                lhsT=xt_codes[:, g, 2 * P * b : 2 * P * (b + 1)].bitcast(FP4X4),
                lhsT_scale=xt_plane[:, g, P * b : P * (b + 1)],
                rhs=codes[head, s, g, half][:, 2 * sub : 2 * (sub + hi - lo)].bitcast(FP4X4),
                rhs_scale=planes[head, s][:, g, lo:hi],
                start=(g == 0),
                stop=(g == GROUPS - 1),
            )

        def new_acc(head, b, c0, c1):
            acc[head, b, c0] = psum.tile([P, BANK], F32, name="bank")

        base = {}
        v_pre = {}
        soft = {}
        for s in range(STRETCHES):
            for b in range(BLOCKS):
                base[s, b] = keep.tile([P, WIDE], F32, name="base%d%d" % (s, b))
                v_pre[s, b] = keep.tile([P, WIDE], F32, name="v_pre%d%d" % (s, b))
                soft[s, b] = keep.tile([P, WIDE], F32, name="soft%d%d" % (s, b))

        def blend_x(s, b, on_scalar):
            if on_scalar:
                nc.scalar.activation(out=base[s, b][:], in_=rows["x", s][:, b, :], func=ACT.Copy, scale=one_minus_t[b][:])
            else:
                nc.gpsimd.tensor_scalar(
                    out=base[s, b][:], in0=rows["x", s][:, b, :], scalar1=one_minus_t[b][:], scalar2=0.0,
                    op0=ALU.mult, op1=ALU.add,
                )

        def blend_bm(s, b):
            nc.vector.scalar_tensor_tensor(
                out=base[s, b][:], in0=bias_all["m"][:, WIDE * s : WIDE * (s + 1)], scalar=t_f32[b][:],
                in1=base[s, b][:], op0=ALU.mult, op1=ALU.add,
            )

        def add_bv(b, c0, c1):
            s, lo = divmod(c0, WIDE)
            nc.vector.tensor_tensor(
                out=v_pre[s, b][:, lo : lo + c1 - c0], in0=acc["v", b, c0][:],
                in1=bias_all["v"][:, c0:c1], op=ALU.add,
            )

        def exp_v(s, b):
            nc.scalar.activation(out=soft[s, b][:], in_=v_pre[s, b][:], func=ACT.Exp)

        def ln_v(s, b):
            nc.scalar.activation(out=soft[s, b][:], in_=soft[s, b][:], func=ACT.Ln, bias=1.0)

        def sigma(s, b):
            nc.vector.scalar_tensor_tensor(
                out=soft[s, b][:], in0=soft[s, b][:], scalar=SOFTPLUS_LINEAR, in1=v_pre[s, b][:],
                op0=ALU.min, op1=ALU.max,
            )

        def noise(s, b):
            nc.vector.scalar_tensor_tensor(
                out=soft[s, b][:], in0=soft[s, b][:], scalar=t_f32[b][:], in1=rows["eps", s][:, b, :],
                op0=ALU.mult, op1=ALU.mult,
            )

        def add_base(s, b, kind):
            engine = nc.vector if kind == "e" else nc.gpsimd
            width = BANK if kind == "g" else WIDE
            for lo in range(0, WIDE, width):
                cols = slice(lo, lo + width)
                engine.tensor_tensor(
                    out=base[s, b][:, cols], in0=soft[s, b][:, cols], in1=base[s, b][:, cols], op=ALU.add
                )

        def finish(b, c0, c1):
            s, lo = divmod(c0, WIDE)
            cols = slice(lo, lo + c1 - c0)
            nc.vector.scalar_tensor_tensor(
                out=base[s, b][:, cols], in0=acc["m", b, c0][:, 0 : c1 - c0], scalar=t_f32[b][:],
                in1=base[s, b][:, cols], op0=ALU.mult, op1=ALU.add,
            )
            nc.sync.dma_start(out=out[P * b : P * (b + 1), c0:c1], in_=base[s, b][:, cols])

        order = []
        for head in "vm":
            for s in range(STRETCHES):
                for c0 in (WIDE * s, WIDE * s + BANK):
                    for b in range(BLOCKS):
                        order.append([(head, b, c0, c0 + BANK)])
        head, b, c0, c1 = order.pop()[0]
        order.append([(head, b, c0, c0 + BANK // 2), (head, b, c0 + BANK // 2, c1)])

        def run(token):
            kind = token[0]
            if kind in "AF":
                for group in order[int(token[1:])]:
                    (add_bv if kind == "A" else finish)(*group[1:])
                return
            s, b = int(token[1]), int(token[2])
            if kind in "xX":
                blend_x(s, b, kind == "x")
            elif kind == "G":
                blend_bm(s, b)
            elif kind == "E":
                exp_v(s, b)
            elif kind == "L":
                ln_v(s, b)
            elif kind == "C":
                sigma(s, b)
            elif kind in "Dd":
                noise(s, b)
            else:
                add_base(s, b, kind)

        for (group,) in order[:4]:
            new_acc(*group)
        for g in range(GROUPS):
            for (group,) in order[:4]:
                mx_pass(*group, g)
        for j in range(3, len(order)):
            if j > 3:
                for group in order[j]:
                    new_acc(*group)
                    for g in range(GROUPS):
                        mx_pass(*group, g)
            for token in STEPS[j].split():
                run(token)
